import numpy as np
import ml_dtypes

BF16 = ml_dtypes.bfloat16


def bf(x):
    return np.asarray(x, np.float32).astype(BF16)


def f32(x):
    return np.asarray(x, np.float32)


def f64(x):
    return np.asarray(x).astype(np.float64)


def striped(idx):
    return np.tile(idx.reshape(-1, 16).T, (8, 1))


C, S, N = 768, 512, 128
LN_EPS = 1e-6


def setup_inputs():
    x = np.random.standard_normal((C, N)) * (0.5 + np.random.rand(1, N)) + 0.5 * np.random.standard_normal((1, N))
    return {"base": f32(np.random.standard_normal((C, S))), "x": f32(x), "ln_a": f32(1.0 + 0.1 * np.random.standard_normal((C, 1))), "ln_b": f32(0.1 * np.random.standard_normal((C, 1))), "offs": striped(np.random.permutation(S)[:N])}


def reference(base, x, ln_a, ln_b, offs):
    idx = offs[:16].T.reshape(-1)
    x = f64(x)
    mean = x.sum(axis=0, keepdims=True) / C
    d = x - mean
    sd = np.sqrt((d * d).sum(axis=0, keepdims=True) / (C - 1))
    t = f64(ln_a) * d / (sd + LN_EPS)
    out = f64(base).copy()
    out[:, idx] = t + f64(ln_b)
    return out

@@ -1,0 +1,96 @@
+import concourse.masks as masks
+import concourse.mybir as mybir
+
+F32 = mybir.dt.float32
+U16 = mybir.dt.uint16
+ALU = mybir.AluOpType
+ACT = mybir.ActivationFunctionType
+
+P = 128
+C, S, N = 768, 512, 128
+BLOCKS = C // P
+HALF = BLOCKS // 2
+LN_EPS = 1e-6
+SQRT_FLOOR = 2.0**-100
+
+
+def tile_daca_kernel(tc, base, x, ln_a, ln_b, offs, out):
+    nc = tc.nc
+    with (
+        tc.tile_pool(name="held", bufs=1) as held,
+        tc.psum_pool(name="psum", bufs=1) as psum,
+        tc.psum_pool(name="psum_back", bufs=4) as psum_back,
+    ):
+        queues = (nc.sync, nc.scalar)
+        x_half = []
+        for h in range(2):
+            xh = held.tile([P, HALF * N], F32, name=f"x_half{h}")
+            queues[h].dma_start(
+                xh[:].rearrange("p (b j) -> p b j", b=HALF),
+                x[h * HALF * P : (h + 1) * HALF * P, :].rearrange("(b p) j -> p b j", p=P),
+            )
+            x_half.append(xh)
+
+        offsets = held.tile([P, N // 16], U16, name="offsets")
+        nc.sync.dma_start(offsets[:], offs)
+
+        ln_rows = held.tile([P, P], F32, name="ln_rows")
+        nc.vector.memset(ln_rows[:], 0.0)
+        nc.sync.dma_start(ln_rows[0:BLOCKS, :], ln_a.rearrange("(b p) o -> b (p o)", p=P))
+        nc.scalar.dma_start(ln_rows[BLOCKS : 2 * BLOCKS, :], ln_b.rearrange("(b p) o -> b (p o)", p=P))
+
+        windows = []
+        for b in range(BLOCKS):
+            window = held.tile([P, S], F32, name=f"window{b}")
+            queues[b % 2].dma_start(window[:], base[b * P : (b + 1) * P, :])
+            windows.append(window)
+
+        identity = held.tile([P, P], F32, name="identity")
+        masks.make_identity(nc, identity[:])
+
+        ln_cols_ps = psum.tile([P, P], F32, name="ln_cols_ps")
+        nc.tensor.transpose(ln_cols_ps[:], ln_rows[:], identity[:])
+        ln_cols = held.tile([P, 2 * BLOCKS], F32, name="ln_cols")
+        nc.vector.tensor_copy(ln_cols[:], ln_cols_ps[:, 0 : 2 * BLOCKS])
+        bias_all = held.tile([P, BLOCKS * N], F32, name="bias_all")
+        nc.gpsimd.tensor_copy(
+            bias_all[:].rearrange("p (b j) -> p b j", b=BLOCKS),
+            ln_cols[:, BLOCKS : 2 * BLOCKS].unsqueeze(2).to_broadcast([P, BLOCKS, N]),
+        )
+
+        stats = held.tile([P, 2 * 6], F32, name="stats")
+        xt_half = []
+        for h in range(2):
+            xt = psum.tile([P, HALF * P], F32, name=f"xt_half{h}")
+            for k in range(HALF):
+                nc.tensor.transpose(xt[:, k * P : (k + 1) * P], x_half[h][:, k * N : (k + 1) * N], identity[:])
+            nc.vector.bn_stats(stats[:, h * 6 : (h + 1) * 6], xt[:])
+            xt_half.append(xt)
+
+        mean_var = held.tile([P, 2], F32, name="mean_var")
+        nc.vector.bn_aggr(mean_var[:], stats[:])
+        mean = mean_var[:, 0:1]
+
+        var_unbiased = held.tile([P, 1], F32, name="var_unbiased")
+        nc.vector.tensor_scalar(var_unbiased[:], mean_var[:, 1:2], C / (C - 1), SQRT_FLOOR, ALU.mult, ALU.max)
+        sd = held.tile([P, 1], F32, name="sd")
+        nc.scalar.activation(sd[:], var_unbiased[:], ACT.Sqrt)
+        sd_eps = held.tile([P, 1], F32, name="sd_eps")
+        nc.vector.tensor_scalar_add(sd_eps[:], sd[:], LN_EPS)
+        rstd = held.tile([P, 1], F32, name="rstd")
+        nc.vector.reciprocal(rstd[:], sd_eps[:])
+        neg_mean_rstd = held.tile([P, 1], F32, name="neg_mean_rstd")
+        nc.vector.tensor_scalar(neg_mean_rstd[:], mean, rstd[:], -1.0, ALU.mult, ALU.mult)
+
+        xn_half = [held.tile([P, HALF * P], F32, name=f"xn_half{h}") for h in range(2)]
+        nc.vector.tensor_scalar(xn_half[0][:], xt_half[0][:], mean, rstd[:], ALU.subtract, ALU.mult)
+        nc.scalar.activation(xn_half[1][:], xt_half[1][:], ACT.Identity, bias=neg_mean_rstd[:], scale=rstd[:])
+
+        for b in range(BLOCKS):
+            h, k = divmod(b, HALF)
+            back = psum_back.tile([P, N], F32, name="back")
+            nc.tensor.transpose(back[:], xn_half[h][:, k * P : (k + 1) * P], identity[:])
+            t = held.tile([P, N], F32, name=f"t{b}")
+            nc.scalar.mul(t[:], back[:], ln_cols[:, b : b + 1])
+            nc.vector.tensor_tensor(windows[b][:].indirect(offsets[:]), t[:], bias_all[:, b * N : (b + 1) * N], ALU.add)
+            nc.sync.dma_start(out[b * P : (b + 1) * P, :], windows[b][:])

@@ -9,7 +9,7 @@ ACT = mybir.ActivationFunctionType
 P = 128
 C, S, N = 768, 512, 128
 BLOCKS = C // P
-HALF = BLOCKS // 2
+PAIRS = BLOCKS // 2
 LN_EPS = 1e-6
 SQRT_FLOOR = 2.0**-100
 
@@ -21,15 +21,14 @@ def tile_daca_kernel(tc, base, x, ln_a, ln_b, offs, out):
         tc.psum_pool(name="psum", bufs=1) as psum,
         tc.psum_pool(name="psum_back", bufs=4) as psum_back,
     ):
-        queues = (nc.sync, nc.scalar)
-        x_half = []
-        for h in range(2):
-            xh = held.tile([P, HALF * N], F32, name=f"x_half{h}")
-            queues[h].dma_start(
-                xh[:].rearrange("p (b j) -> p b j", b=HALF),
-                x[h * HALF * P : (h + 1) * HALF * P, :].rearrange("(b p) j -> p b j", p=P),
+        x_pair = []
+        for q in range(PAIRS):
+            xq = held.tile([P, 2 * N], F32, name=f"x_pair{q}")
+            nc.sync.dma_start(
+                xq[:].rearrange("p (b j) -> p b j", b=2),
+                x[q * 2 * P : (q + 1) * 2 * P, :].rearrange("(b p) j -> p b j", p=P),
             )
-            x_half.append(xh)
+            x_pair.append(xq)
 
         offsets = held.tile([P, N // 16], U16, name="offsets")
         nc.sync.dma_start(offsets[:], offs)
@@ -37,59 +36,63 @@ def tile_daca_kernel(tc, base, x, ln_a, ln_b, offs, out):
         ln_rows = held.tile([P, P], F32, name="ln_rows")
         nc.vector.memset(ln_rows[:], 0.0)
         nc.sync.dma_start(ln_rows[0:BLOCKS, :], ln_a.rearrange("(b p) o -> b (p o)", p=P))
-        nc.scalar.dma_start(ln_rows[BLOCKS : 2 * BLOCKS, :], ln_b.rearrange("(b p) o -> b (p o)", p=P))
+        nc.sync.dma_start(ln_rows[BLOCKS : 2 * BLOCKS, :], ln_b.rearrange("(b p) o -> b (p o)", p=P))
 
         windows = []
         for b in range(BLOCKS):
             window = held.tile([P, S], F32, name=f"window{b}")
-            queues[b % 2].dma_start(window[:], base[b * P : (b + 1) * P, :])
+            nc.sync.dma_start(window[:], base[b * P : (b + 1) * P, :])
             windows.append(window)
 
         identity = held.tile([P, P], F32, name="identity")
         masks.make_identity(nc, identity[:])
+        sqrt_floor = held.tile([P, 1], F32, name="sqrt_floor")
+        nc.vector.memset(sqrt_floor[:], SQRT_FLOOR)
+
+        stats = held.tile([P, PAIRS * 6], F32, name="stats")
+        xt_pair = []
+        for q in range(PAIRS):
+            xt = psum.tile([P, 2 * P], F32, name=f"xt_pair{q}")
+            for k in range(2):
+                nc.tensor.transpose(xt[:, k * P : (k + 1) * P], x_pair[q][:, k * N : (k + 1) * N], identity[:])
+            nc.vector.bn_stats(stats[:, q * 6 : (q + 1) * 6], xt[:])
+            xt_pair.append(xt)
+
+        mean_var = held.tile([P, 2], F32, name="mean_var")
+        nc.vector.bn_aggr(mean_var[:], stats[:])
+        mean = mean_var[:, 0:1]
+
+        sd = held.tile([P, 1], F32, name="sd")
+        nc.scalar.activation(sd[:], mean_var[:, 1:2], ACT.Sqrt, bias=sqrt_floor[:], scale=C / (C - 1))
+        sd_eps = held.tile([P, 1], F32, name="sd_eps")
+        nc.vector.tensor_scalar_add(sd_eps[:], sd[:], LN_EPS)
+        rstd = held.tile([P, 1], F32, name="rstd")
+        nc.vector.reciprocal(rstd[:], sd_eps[:])
 
         ln_cols_ps = psum.tile([P, P], F32, name="ln_cols_ps")
         nc.tensor.transpose(ln_cols_ps[:], ln_rows[:], identity[:])
         ln_cols = held.tile([P, 2 * BLOCKS], F32, name="ln_cols")
-        nc.vector.tensor_copy(ln_cols[:], ln_cols_ps[:, 0 : 2 * BLOCKS])
+        nc.scalar.copy(ln_cols[:], ln_cols_ps[:, 0 : 2 * BLOCKS])
         bias_all = held.tile([P, BLOCKS * N], F32, name="bias_all")
         nc.gpsimd.tensor_copy(
             bias_all[:].rearrange("p (b j) -> p b j", b=BLOCKS),
             ln_cols[:, BLOCKS : 2 * BLOCKS].unsqueeze(2).to_broadcast([P, BLOCKS, N]),
         )
 
-        stats = held.tile([P, 2 * 6], F32, name="stats")
-        xt_half = []
-        for h in range(2):
-            xt = psum.tile([P, HALF * P], F32, name=f"xt_half{h}")
-            for k in range(HALF):
-                nc.tensor.transpose(xt[:, k * P : (k + 1) * P], x_half[h][:, k * N : (k + 1) * N], identity[:])
-            nc.vector.bn_stats(stats[:, h * 6 : (h + 1) * 6], xt[:])
-            xt_half.append(xt)
-
-        mean_var = held.tile([P, 2], F32, name="mean_var")
-        nc.vector.bn_aggr(mean_var[:], stats[:])
-        mean = mean_var[:, 0:1]
-
-        var_unbiased = held.tile([P, 1], F32, name="var_unbiased")
-        nc.vector.tensor_scalar(var_unbiased[:], mean_var[:, 1:2], C / (C - 1), SQRT_FLOOR, ALU.mult, ALU.max)
-        sd = held.tile([P, 1], F32, name="sd")
-        nc.scalar.activation(sd[:], var_unbiased[:], ACT.Sqrt)
-        sd_eps = held.tile([P, 1], F32, name="sd_eps")
-        nc.vector.tensor_scalar_add(sd_eps[:], sd[:], LN_EPS)
-        rstd = held.tile([P, 1], F32, name="rstd")
-        nc.vector.reciprocal(rstd[:], sd_eps[:])
+        xn_pair = [held.tile([P, 2 * P], F32, name=f"xn_pair{q}") for q in range(PAIRS)]
+        nc.vector.tensor_scalar(xn_pair[0][:, 0:P], xt_pair[0][:, 0:P], mean, rstd[:], ALU.subtract, ALU.mult)
         neg_mean_rstd = held.tile([P, 1], F32, name="neg_mean_rstd")
         nc.vector.tensor_scalar(neg_mean_rstd[:], mean, rstd[:], -1.0, ALU.mult, ALU.mult)
-
-        xn_half = [held.tile([P, HALF * P], F32, name=f"xn_half{h}") for h in range(2)]
-        nc.vector.tensor_scalar(xn_half[0][:], xt_half[0][:], mean, rstd[:], ALU.subtract, ALU.mult)
-        nc.scalar.activation(xn_half[1][:], xt_half[1][:], ACT.Identity, bias=neg_mean_rstd[:], scale=rstd[:])
+        nc.scalar.activation(xn_pair[2][:], xt_pair[2][:], ACT.Identity, bias=neg_mean_rstd[:], scale=rstd[:])
+        for b in range(1, 4):
+            q, k = divmod(b, 2)
+            cols = slice(k * P, (k + 1) * P)
+            nc.vector.tensor_scalar(xn_pair[q][:, cols], xt_pair[q][:, cols], mean, rstd[:], ALU.subtract, ALU.mult)
 
         for b in range(BLOCKS):
-            h, k = divmod(b, HALF)
+            q, k = divmod(b, 2)
             back = psum_back.tile([P, N], F32, name="back")
-            nc.tensor.transpose(back[:], xn_half[h][:, k * P : (k + 1) * P], identity[:])
+            nc.tensor.transpose(back[:], xn_pair[q][:, k * P : (k + 1) * P], identity[:])
             t = held.tile([P, N], F32, name=f"t{b}")
             nc.scalar.mul(t[:], back[:], ln_cols[:, b : b + 1])
             nc.vector.tensor_tensor(windows[b][:].indirect(offsets[:]), t[:], bias_all[:, b * N : (b + 1) * N], ALU.add)

@@ -9,7 +9,7 @@ ACT = mybir.ActivationFunctionType
 P = 128
 C, S, N = 768, 512, 128
 BLOCKS = C // P
-PAIRS = BLOCKS // 2
+PIECES = (3, 2, 1)
 LN_EPS = 1e-6
 SQRT_FLOOR = 2.0**-100
 
@@ -21,14 +21,16 @@ def tile_daca_kernel(tc, base, x, ln_a, ln_b, offs, out):
         tc.psum_pool(name="psum", bufs=1) as psum,
         tc.psum_pool(name="psum_back", bufs=4) as psum_back,
     ):
-        x_pair = []
-        for q in range(PAIRS):
-            xq = held.tile([P, 2 * N], F32, name=f"x_pair{q}")
+        x_blocks = []
+        first = 0
+        for q, blocks in enumerate(PIECES):
+            x_piece = held.tile([P, blocks * N], F32, name=f"x_piece{q}")
             nc.sync.dma_start(
-                xq[:].rearrange("p (b j) -> p b j", b=2),
-                x[q * 2 * P : (q + 1) * 2 * P, :].rearrange("(b p) j -> p b j", p=P),
+                x_piece[:].rearrange("p (b j) -> p b j", b=blocks),
+                x[first * P : (first + blocks) * P, :].rearrange("(b p) j -> p b j", p=P),
             )
-            x_pair.append(xq)
+            x_blocks += [x_piece[:, k * N : (k + 1) * N] for k in range(blocks)]
+            first += blocks
 
         offsets = held.tile([P, N // 16], U16, name="offsets")
         nc.sync.dma_start(offsets[:], offs)
@@ -49,14 +51,15 @@ def tile_daca_kernel(tc, base, x, ln_a, ln_b, offs, out):
         sqrt_floor = held.tile([P, 1], F32, name="sqrt_floor")
         nc.vector.memset(sqrt_floor[:], SQRT_FLOOR)
 
-        stats = held.tile([P, PAIRS * 6], F32, name="stats")
-        xt_pair = []
-        for q in range(PAIRS):
-            xt = psum.tile([P, 2 * P], F32, name=f"xt_pair{q}")
-            for k in range(2):
-                nc.tensor.transpose(xt[:, k * P : (k + 1) * P], x_pair[q][:, k * N : (k + 1) * N], identity[:])
-            nc.vector.bn_stats(stats[:, q * 6 : (q + 1) * 6], xt[:])
-            xt_pair.append(xt)
+        stats = held.tile([P, len(PIECES) * 6], F32, name="stats")
+        xt_blocks = []
+        for q, blocks in enumerate(PIECES):
+            xt_piece = psum.tile([P, blocks * P], F32, name=f"xt_piece{q}")
+            for k in range(blocks):
+                xt_block = xt_piece[:, k * P : (k + 1) * P]
+                nc.tensor.transpose(xt_block, x_blocks[len(xt_blocks)], identity[:])
+                xt_blocks.append(xt_block)
+            nc.vector.bn_stats(stats[:, q * 6 : (q + 1) * 6], xt_piece[:])
 
         mean_var = held.tile([P, 2], F32, name="mean_var")
         nc.vector.bn_aggr(mean_var[:], stats[:])
@@ -79,20 +82,18 @@ def tile_daca_kernel(tc, base, x, ln_a, ln_b, offs, out):
             ln_cols[:, BLOCKS : 2 * BLOCKS].unsqueeze(2).to_broadcast([P, BLOCKS, N]),
         )
 
-        xn_pair = [held.tile([P, 2 * P], F32, name=f"xn_pair{q}") for q in range(PAIRS)]
-        nc.vector.tensor_scalar(xn_pair[0][:, 0:P], xt_pair[0][:, 0:P], mean, rstd[:], ALU.subtract, ALU.mult)
+        xn_blocks = [held.tile([P, P], F32, name=f"xn{b}") for b in range(BLOCKS)]
+        nc.vector.tensor_scalar(xn_blocks[0][:], xt_blocks[0], mean, rstd[:], ALU.subtract, ALU.mult)
         neg_mean_rstd = held.tile([P, 1], F32, name="neg_mean_rstd")
         nc.vector.tensor_scalar(neg_mean_rstd[:], mean, rstd[:], -1.0, ALU.mult, ALU.mult)
-        nc.scalar.activation(xn_pair[2][:], xt_pair[2][:], ACT.Identity, bias=neg_mean_rstd[:], scale=rstd[:])
-        for b in range(1, 4):
-            q, k = divmod(b, 2)
-            cols = slice(k * P, (k + 1) * P)
-            nc.vector.tensor_scalar(xn_pair[q][:, cols], xt_pair[q][:, cols], mean, rstd[:], ALU.subtract, ALU.mult)
+        last = BLOCKS - 1
+        nc.scalar.activation(xn_blocks[last][:], xt_blocks[last], ACT.Identity, bias=neg_mean_rstd[:], scale=rstd[:])
+        for b in range(1, last):
+            nc.vector.tensor_scalar(xn_blocks[b][:], xt_blocks[b], mean, rstd[:], ALU.subtract, ALU.mult)
 
         for b in range(BLOCKS):
-            q, k = divmod(b, 2)
             back = psum_back.tile([P, N], F32, name="back")
-            nc.tensor.transpose(back[:], xn_pair[q][:, k * P : (k + 1) * P], identity[:])
+            nc.tensor.transpose(back[:], xn_blocks[b][:], identity[:])
             t = held.tile([P, N], F32, name=f"t{b}")
             nc.scalar.mul(t[:], back[:], ln_cols[:, b : b + 1])
             nc.vector.tensor_tensor(windows[b][:].indirect(offsets[:]), t[:], bias_all[:, b * N : (b + 1) * N], ALU.add)

@@ -9,41 +9,40 @@ ACT = mybir.ActivationFunctionType
 P = 128
 C, S, N = 768, 512, 128
 BLOCKS = C // P
-PIECES = (3, 2, 1)
+PAIRS = BLOCKS // 2
 LN_EPS = 1e-6
 SQRT_FLOOR = 2.0**-100
 
 
 def tile_daca_kernel(tc, base, x, ln_a, ln_b, offs, out):
     nc = tc.nc
+    x_view = x.rearrange("(p b) j -> p b j", b=BLOCKS)
+    base_view = base.rearrange("(p b) s -> p b s", b=BLOCKS)
+    out_view = out.rearrange("(p b) s -> p b s", b=BLOCKS)
+
     with (
         tc.tile_pool(name="held", bufs=1) as held,
         tc.psum_pool(name="psum", bufs=1) as psum,
         tc.psum_pool(name="psum_back", bufs=4) as psum_back,
     ):
-        x_blocks = []
-        first = 0
-        for q, blocks in enumerate(PIECES):
-            x_piece = held.tile([P, blocks * N], F32, name=f"x_piece{q}")
-            nc.sync.dma_start(
-                x_piece[:].rearrange("p (b j) -> p b j", b=blocks),
-                x[first * P : (first + blocks) * P, :].rearrange("(b p) j -> p b j", p=P),
-            )
-            x_blocks += [x_piece[:, k * N : (k + 1) * N] for k in range(blocks)]
-            first += blocks
+        x_pair = []
+        for q in range(PAIRS):
+            xq = held.tile([P, 2 * N], F32, name=f"x_pair{q}")
+            nc.sync.dma_start(xq[:].rearrange("p (b j) -> p b j", b=2), x_view[:, 2 * q : 2 * q + 2, :])
+            x_pair.append(xq)
 
         offsets = held.tile([P, N // 16], U16, name="offsets")
         nc.sync.dma_start(offsets[:], offs)
 
-        ln_rows = held.tile([P, P], F32, name="ln_rows")
-        nc.vector.memset(ln_rows[:], 0.0)
-        nc.sync.dma_start(ln_rows[0:BLOCKS, :], ln_a.rearrange("(b p) o -> b (p o)", p=P))
-        nc.sync.dma_start(ln_rows[BLOCKS : 2 * BLOCKS, :], ln_b.rearrange("(b p) o -> b (p o)", p=P))
+        gain = held.tile([P, BLOCKS], F32, name="gain")
+        nc.sync.dma_start(gain[:], ln_a.rearrange("(p b) o -> p (b o)", b=BLOCKS))
+        bias = held.tile([P, BLOCKS], F32, name="bias")
+        nc.sync.dma_start(bias[:], ln_b.rearrange("(p b) o -> p (b o)", b=BLOCKS))
 
         windows = []
         for b in range(BLOCKS):
             window = held.tile([P, S], F32, name=f"window{b}")
-            nc.sync.dma_start(window[:], base[b * P : (b + 1) * P, :])
+            nc.sync.dma_start(window[:], base_view[:, b, :])
             windows.append(window)
 
         identity = held.tile([P, P], F32, name="identity")
@@ -51,15 +50,20 @@ def tile_daca_kernel(tc, base, x, ln_a, ln_b, offs, out):
         sqrt_floor = held.tile([P, 1], F32, name="sqrt_floor")
         nc.vector.memset(sqrt_floor[:], SQRT_FLOOR)
 
-        stats = held.tile([P, len(PIECES) * 6], F32, name="stats")
-        xt_blocks = []
-        for q, blocks in enumerate(PIECES):
-            xt_piece = psum.tile([P, blocks * P], F32, name=f"xt_piece{q}")
-            for k in range(blocks):
-                xt_block = xt_piece[:, k * P : (k + 1) * P]
-                nc.tensor.transpose(xt_block, x_blocks[len(xt_blocks)], identity[:])
-                xt_blocks.append(xt_block)
-            nc.vector.bn_stats(stats[:, q * 6 : (q + 1) * 6], xt_piece[:])
+        bias_all = held.tile([P, BLOCKS * N], F32, name="bias_all")
+        nc.gpsimd.tensor_copy(
+            bias_all[:].rearrange("p (b j) -> p b j", b=BLOCKS),
+            bias[:].unsqueeze(2).to_broadcast([P, BLOCKS, N]),
+        )
+
+        stats = held.tile([P, PAIRS * 6], F32, name="stats")
+        xt_pair = []
+        for q in range(PAIRS):
+            xt = psum.tile([P, 2 * P], F32, name=f"xt_pair{q}")
+            for k in range(2):
+                nc.tensor.transpose(xt[:, k * P : (k + 1) * P], x_pair[q][:, k * N : (k + 1) * N], identity[:])
+            nc.vector.bn_stats(stats[:, q * 6 : (q + 1) * 6], xt[:])
+            xt_pair.append(xt)
 
         mean_var = held.tile([P, 2], F32, name="mean_var")
         nc.vector.bn_aggr(mean_var[:], stats[:])
@@ -72,29 +76,21 @@ def tile_daca_kernel(tc, base, x, ln_a, ln_b, offs, out):
         rstd = held.tile([P, 1], F32, name="rstd")
         nc.vector.reciprocal(rstd[:], sd_eps[:])
 
-        ln_cols_ps = psum.tile([P, P], F32, name="ln_cols_ps")
-        nc.tensor.transpose(ln_cols_ps[:], ln_rows[:], identity[:])
-        ln_cols = held.tile([P, 2 * BLOCKS], F32, name="ln_cols")
-        nc.scalar.copy(ln_cols[:], ln_cols_ps[:, 0 : 2 * BLOCKS])
-        bias_all = held.tile([P, BLOCKS * N], F32, name="bias_all")
-        nc.gpsimd.tensor_copy(
-            bias_all[:].rearrange("p (b j) -> p b j", b=BLOCKS),
-            ln_cols[:, BLOCKS : 2 * BLOCKS].unsqueeze(2).to_broadcast([P, BLOCKS, N]),
-        )
-
-        xn_blocks = [held.tile([P, P], F32, name=f"xn{b}") for b in range(BLOCKS)]
-        nc.vector.tensor_scalar(xn_blocks[0][:], xt_blocks[0], mean, rstd[:], ALU.subtract, ALU.mult)
+        xn_pair = [held.tile([P, 2 * P], F32, name=f"xn_pair{q}") for q in range(PAIRS)]
+        nc.vector.tensor_scalar(xn_pair[0][:, 0:P], xt_pair[0][:, 0:P], mean, rstd[:], ALU.subtract, ALU.mult)
         neg_mean_rstd = held.tile([P, 1], F32, name="neg_mean_rstd")
         nc.vector.tensor_scalar(neg_mean_rstd[:], mean, rstd[:], -1.0, ALU.mult, ALU.mult)
-        last = BLOCKS - 1
-        nc.scalar.activation(xn_blocks[last][:], xt_blocks[last], ACT.Identity, bias=neg_mean_rstd[:], scale=rstd[:])
-        for b in range(1, last):
-            nc.vector.tensor_scalar(xn_blocks[b][:], xt_blocks[b], mean, rstd[:], ALU.subtract, ALU.mult)
+        nc.scalar.activation(xn_pair[2][:], xt_pair[2][:], ACT.Identity, bias=neg_mean_rstd[:], scale=rstd[:])
+        for b in range(1, 4):
+            q, k = divmod(b, 2)
+            cols = slice(k * P, (k + 1) * P)
+            nc.vector.tensor_scalar(xn_pair[q][:, cols], xt_pair[q][:, cols], mean, rstd[:], ALU.subtract, ALU.mult)
 
         for b in range(BLOCKS):
+            q, k = divmod(b, 2)
             back = psum_back.tile([P, N], F32, name="back")
-            nc.tensor.transpose(back[:], xn_blocks[b][:], identity[:])
+            nc.tensor.transpose(back[:], xn_pair[q][:, k * P : (k + 1) * P], identity[:])
             t = held.tile([P, N], F32, name=f"t{b}")
-            nc.scalar.mul(t[:], back[:], ln_cols[:, b : b + 1])
+            nc.scalar.mul(t[:], back[:], gain[:, b : b + 1])
             nc.vector.tensor_tensor(windows[b][:].indirect(offsets[:]), t[:], bias_all[:, b * N : (b + 1) * N], ALU.add)
-            nc.sync.dma_start(out[b * P : (b + 1) * P, :], windows[b][:])
+            nc.sync.dma_start(out_view[:, b, :], windows[b][:])

@@ -76,20 +76,16 @@ def tile_daca_kernel(tc, base, x, ln_a, ln_b, offs, out):
         rstd = held.tile([P, 1], F32, name="rstd")
         nc.vector.reciprocal(rstd[:], sd_eps[:])
 
-        xn_pair = [held.tile([P, 2 * P], F32, name=f"xn_pair{q}") for q in range(PAIRS)]
-        nc.vector.tensor_scalar(xn_pair[0][:, 0:P], xt_pair[0][:, 0:P], mean, rstd[:], ALU.subtract, ALU.mult)
-        neg_mean_rstd = held.tile([P, 1], F32, name="neg_mean_rstd")
-        nc.vector.tensor_scalar(neg_mean_rstd[:], mean, rstd[:], -1.0, ALU.mult, ALU.mult)
-        nc.scalar.activation(xn_pair[2][:], xt_pair[2][:], ACT.Identity, bias=neg_mean_rstd[:], scale=rstd[:])
-        for b in range(1, 4):
-            q, k = divmod(b, 2)
-            cols = slice(k * P, (k + 1) * P)
-            nc.vector.tensor_scalar(xn_pair[q][:, cols], xt_pair[q][:, cols], mean, rstd[:], ALU.subtract, ALU.mult)
-
+        xn_blocks = []
         for b in range(BLOCKS):
             q, k = divmod(b, 2)
+            xn = held.tile([P, P], F32, name=f"xn{b}")
+            nc.vector.tensor_scalar(xn[:], xt_pair[q][:, k * P : (k + 1) * P], mean, rstd[:], ALU.subtract, ALU.mult)
+            xn_blocks.append(xn)
+
+        for b in range(BLOCKS):
             back = psum_back.tile([P, N], F32, name="back")
-            nc.tensor.transpose(back[:], xn_pair[q][:, k * P : (k + 1) * P], identity[:])
+            nc.tensor.transpose(back[:], xn_blocks[b][:], identity[:])
             t = held.tile([P, N], F32, name=f"t{b}")
             nc.scalar.mul(t[:], back[:], gain[:, b : b + 1])
             nc.vector.tensor_tensor(windows[b][:].indirect(offsets[:]), t[:], bias_all[:, b * N : (b + 1) * N], ALU.add)

@@ -34,10 +34,10 @@ def tile_daca_kernel(tc, base, x, ln_a, ln_b, offs, out):
         offsets = held.tile([P, N // 16], U16, name="offsets")
         nc.sync.dma_start(offsets[:], offs)
 
-        gain = held.tile([P, BLOCKS], F32, name="gain")
-        nc.sync.dma_start(gain[:], ln_a.rearrange("(p b) o -> p (b o)", b=BLOCKS))
         bias = held.tile([P, BLOCKS], F32, name="bias")
-        nc.sync.dma_start(bias[:], ln_b.rearrange("(p b) o -> p (b o)", b=BLOCKS))
+        nc.scalar.dma_start(bias[:], ln_b.rearrange("(p b) o -> p (b o)", b=BLOCKS))
+        gain = held.tile([P, BLOCKS], F32, name="gain")
+        nc.scalar.dma_start(gain[:], ln_a.rearrange("(p b) o -> p (b o)", b=BLOCKS))
 
         windows = []
         for b in range(BLOCKS):
@@ -51,7 +51,7 @@ def tile_daca_kernel(tc, base, x, ln_a, ln_b, offs, out):
         nc.vector.memset(sqrt_floor[:], SQRT_FLOOR)
 
         bias_all = held.tile([P, BLOCKS * N], F32, name="bias_all")
-        nc.gpsimd.tensor_copy(
+        nc.vector.tensor_copy(
             bias_all[:].rearrange("p (b j) -> p b j", b=BLOCKS),
             bias[:].unsqueeze(2).to_broadcast([P, BLOCKS, N]),
         )

@@ -65,14 +65,16 @@ def tile_daca_kernel(tc, base, x, ln_a, ln_b, offs, out):
             nc.vector.bn_stats(stats[:, q * 6 : (q + 1) * 6], xt[:])
             xt_pair.append(xt)
 
-        mean_var = held.tile([P, 2], F32, name="mean_var")
-        nc.vector.bn_aggr(mean_var[:], stats[:])
-        mean = mean_var[:, 0:1]
+        mean_var_eps = held.tile([P, 3], F32, name="mean_var_eps")
+        nc.vector.memset(mean_var_eps[:, 2:3], LN_EPS * LN_EPS * (C - 1) / C)
+        nc.vector.bn_aggr(mean_var_eps[:, 0:2], stats[:])
+        mean = mean_var_eps[:, 0:1]
 
-        sd = held.tile([P, 1], F32, name="sd")
-        nc.scalar.activation(sd[:], mean_var[:, 1:2], ACT.Sqrt, bias=sqrt_floor[:], scale=C / (C - 1))
+        roots = held.tile([P, 2], F32, name="roots")
         sd_eps = held.tile([P, 1], F32, name="sd_eps")
-        nc.vector.tensor_scalar_add(sd_eps[:], sd[:], LN_EPS)
+        nc.scalar.activation(
+            roots[:], mean_var_eps[:, 1:3], ACT.Sqrt, bias=sqrt_floor[:], scale=C / (C - 1), accum_out=sd_eps[:]
+        )
         rstd = held.tile([P, 1], F32, name="rstd")
         nc.vector.reciprocal(rstd[:], sd_eps[:])
 

@@ -10,6 +10,7 @@ P = 128
 C, S, N = 768, 512, 128
 BLOCKS = C // P
 PAIRS = BLOCKS // 2
+STAT_GROUPS = (2, 2, 1, 1)
 LN_EPS = 1e-6
 SQRT_FLOOR = 2.0**-100
 
@@ -56,14 +57,15 @@ def tile_daca_kernel(tc, base, x, ln_a, ln_b, offs, out):
             bias[:].unsqueeze(2).to_broadcast([P, BLOCKS, N]),
         )
 
-        stats = held.tile([P, PAIRS * 6], F32, name="stats")
-        xt_pair = []
-        for q in range(PAIRS):
-            xt = psum.tile([P, 2 * P], F32, name=f"xt_pair{q}")
-            for k in range(2):
-                nc.tensor.transpose(xt[:, k * P : (k + 1) * P], x_pair[q][:, k * N : (k + 1) * N], identity[:])
-            nc.vector.bn_stats(stats[:, q * 6 : (q + 1) * 6], xt[:])
-            xt_pair.append(xt)
+        stats = held.tile([P, len(STAT_GROUPS) * 6], F32, name="stats")
+        xt_blocks = []
+        for g, width in enumerate(STAT_GROUPS):
+            xt = psum.tile([P, width * P], F32, name=f"xt_group{g}")
+            for k in range(width):
+                q, h = divmod(len(xt_blocks), 2)
+                nc.tensor.transpose(xt[:, k * P : (k + 1) * P], x_pair[q][:, h * N : (h + 1) * N], identity[:])
+                xt_blocks.append(xt[:, k * P : (k + 1) * P])
+            nc.vector.bn_stats(stats[:, g * 6 : (g + 1) * 6], xt[:])
 
         mean_var_eps = held.tile([P, 3], F32, name="mean_var_eps")
         nc.vector.memset(mean_var_eps[:, 2:3], LN_EPS * LN_EPS * (C - 1) / C)
@@ -80,9 +82,8 @@ def tile_daca_kernel(tc, base, x, ln_a, ln_b, offs, out):
 
         xn_blocks = []
         for b in range(BLOCKS):
-            q, k = divmod(b, 2)
             xn = held.tile([P, P], F32, name=f"xn{b}")
-            nc.vector.tensor_scalar(xn[:], xt_pair[q][:, k * P : (k + 1) * P], mean, rstd[:], ALU.subtract, ALU.mult)
+            nc.vector.tensor_scalar(xn[:], xt_blocks[b], mean, rstd[:], ALU.subtract, ALU.mult)
             xn_blocks.append(xn)
 
         for b in range(BLOCKS):

@@ -11,6 +11,7 @@ C, S, N = 768, 512, 128
 BLOCKS = C // P
 PAIRS = BLOCKS // 2
 STAT_GROUPS = (2, 2, 1, 1)
+VECTOR_BLOCKS = 2
 LN_EPS = 1e-6
 SQRT_FLOOR = 2.0**-100
 
@@ -72,6 +73,8 @@ def tile_daca_kernel(tc, base, x, ln_a, ln_b, offs, out):
         nc.vector.bn_aggr(mean_var_eps[:, 0:2], stats[:])
         mean = mean_var_eps[:, 0:1]
 
+        neg_mean = held.tile([P, 1], F32, name="neg_mean")
+        nc.vector.tensor_scalar_mul(neg_mean[:], mean, -1.0)
         roots = held.tile([P, 2], F32, name="roots")
         sd_eps = held.tile([P, 1], F32, name="sd_eps")
         nc.scalar.activation(
@@ -80,16 +83,25 @@ def tile_daca_kernel(tc, base, x, ln_a, ln_b, offs, out):
         rstd = held.tile([P, 1], F32, name="rstd")
         nc.vector.reciprocal(rstd[:], sd_eps[:])
 
+        shift = held.tile([P, 1], F32, name="shift")
+        nc.scalar.mul(shift[:], neg_mean[:], rstd[:])
+
         xn_blocks = []
         for b in range(BLOCKS):
             xn = held.tile([P, P], F32, name=f"xn{b}")
-            nc.vector.tensor_scalar(xn[:], xt_blocks[b], mean, rstd[:], ALU.subtract, ALU.mult)
+            if b < VECTOR_BLOCKS:
+                nc.vector.tensor_scalar(xn[:], xt_blocks[b], mean, rstd[:], ALU.subtract, ALU.mult)
+            else:
+                nc.scalar.activation(xn[:], xt_blocks[b], ACT.Identity, bias=shift[:], scale=rstd[:])
             xn_blocks.append(xn)
 
         for b in range(BLOCKS):
             back = psum_back.tile([P, N], F32, name="back")
             nc.tensor.transpose(back[:], xn_blocks[b][:], identity[:])
             t = held.tile([P, N], F32, name=f"t{b}")
-            nc.scalar.mul(t[:], back[:], gain[:, b : b + 1])
+            if b == 0:
+                nc.vector.tensor_scalar_mul(t[:], back[:], gain[:, b : b + 1])
+            else:
+                nc.scalar.mul(t[:], back[:], gain[:, b : b + 1])
             nc.vector.tensor_tensor(windows[b][:].indirect(offsets[:]), t[:], bias_all[:, b * N : (b + 1) * N], ALU.add)
             nc.sync.dma_start(out_view[:, b, :], windows[b][:])

import concourse.masks as masks
import concourse.mybir as mybir

F32 = mybir.dt.float32
U16 = mybir.dt.uint16
ALU = mybir.AluOpType
ACT = mybir.ActivationFunctionType

P = 128
C, S, N = 768, 512, 128
BLOCKS = C // P
PAIRS = BLOCKS // 2
STAT_GROUPS = (2, 2, 1, 1)
VECTOR_BLOCKS = 2
LN_EPS = 1e-6
SQRT_FLOOR = 2.0**-100


def tile_daca_kernel(tc, base, x, ln_a, ln_b, offs, out):
    nc = tc.nc
    x_view = x.rearrange("(p b) j -> p b j", b=BLOCKS)
    base_view = base.rearrange("(p b) s -> p b s", b=BLOCKS)
    out_view = out.rearrange("(p b) s -> p b s", b=BLOCKS)

    with (
        tc.tile_pool(name="held", bufs=1) as held,
        tc.psum_pool(name="psum", bufs=1) as psum,
        tc.psum_pool(name="psum_back", bufs=4) as psum_back,
    ):
        x_pair = []
        for q in range(PAIRS):
            xq = held.tile([P, 2 * N], F32, name=f"x_pair{q}")
            nc.sync.dma_start(xq[:].rearrange("p (b j) -> p b j", b=2), x_view[:, 2 * q : 2 * q + 2, :])
            x_pair.append(xq)

        offsets = held.tile([P, N // 16], U16, name="offsets")
        nc.sync.dma_start(offsets[:], offs)

        bias = held.tile([P, BLOCKS], F32, name="bias")
        nc.scalar.dma_start(bias[:], ln_b.rearrange("(p b) o -> p (b o)", b=BLOCKS))
        gain = held.tile([P, BLOCKS], F32, name="gain")
        nc.scalar.dma_start(gain[:], ln_a.rearrange("(p b) o -> p (b o)", b=BLOCKS))

        windows = []
        for b in range(BLOCKS):
            window = held.tile([P, S], F32, name=f"window{b}")
            nc.sync.dma_start(window[:], base_view[:, b, :])
            windows.append(window)

        identity = held.tile([P, P], F32, name="identity")
        masks.make_identity(nc, identity[:])
        sqrt_floor = held.tile([P, 1], F32, name="sqrt_floor")
        nc.vector.memset(sqrt_floor[:], SQRT_FLOOR)

        bias_all = held.tile([P, BLOCKS * N], F32, name="bias_all")
        nc.vector.tensor_copy(
            bias_all[:].rearrange("p (b j) -> p b j", b=BLOCKS),
            bias[:].unsqueeze(2).to_broadcast([P, BLOCKS, N]),
        )

        stats = held.tile([P, len(STAT_GROUPS) * 6], F32, name="stats")
        xt_blocks = []
        for g, width in enumerate(STAT_GROUPS):
            xt = psum.tile([P, width * P], F32, name=f"xt_group{g}")
            for k in range(width):
                q, h = divmod(len(xt_blocks), 2)
                nc.tensor.transpose(xt[:, k * P : (k + 1) * P], x_pair[q][:, h * N : (h + 1) * N], identity[:])
                xt_blocks.append(xt[:, k * P : (k + 1) * P])
            nc.vector.bn_stats(stats[:, g * 6 : (g + 1) * 6], xt[:])

        mean_var_eps = held.tile([P, 3], F32, name="mean_var_eps")
        nc.vector.memset(mean_var_eps[:, 2:3], LN_EPS * LN_EPS * (C - 1) / C)
        nc.vector.bn_aggr(mean_var_eps[:, 0:2], stats[:])
        mean = mean_var_eps[:, 0:1]

        neg_mean = held.tile([P, 1], F32, name="neg_mean")
        nc.vector.tensor_scalar_mul(neg_mean[:], mean, -1.0)
        roots = held.tile([P, 2], F32, name="roots")
        sd_eps = held.tile([P, 1], F32, name="sd_eps")
        nc.scalar.activation(
            roots[:], mean_var_eps[:, 1:3], ACT.Sqrt, bias=sqrt_floor[:], scale=C / (C - 1), accum_out=sd_eps[:]
        )
        rstd = held.tile([P, 1], F32, name="rstd")
        nc.vector.reciprocal(rstd[:], sd_eps[:])

        shift = held.tile([P, 1], F32, name="shift")
        nc.scalar.mul(shift[:], neg_mean[:], rstd[:])

        xn_blocks = []
        for b in range(BLOCKS):
            xn = held.tile([P, P], F32, name=f"xn{b}")
            if b < VECTOR_BLOCKS:
                nc.vector.tensor_scalar(xn[:], xt_blocks[b], mean, rstd[:], ALU.subtract, ALU.mult)
            else:
                nc.scalar.activation(xn[:], xt_blocks[b], ACT.Identity, bias=shift[:], scale=rstd[:])
            xn_blocks.append(xn)

        for b in range(BLOCKS):
            back = psum_back.tile([P, N], F32, name="back")
            nc.tensor.transpose(back[:], xn_blocks[b][:], identity[:])
            t = held.tile([P, N], F32, name=f"t{b}")
            if b == 0:
                nc.vector.tensor_scalar_mul(t[:], back[:], gain[:, b : b + 1])
            else:
                nc.scalar.mul(t[:], back[:], gain[:, b : b + 1])
            nc.vector.tensor_tensor(windows[b][:].indirect(offsets[:]), t[:], bias_all[:, b * N : (b + 1) * N], ALU.add)
            nc.sync.dma_start(out_view[:, b, :], windows[b][:])
